import numpy as np
import ml_dtypes


def mxq(x, axis, fmt="e4m3"):
    dtype, down = {"e4m3": (ml_dtypes.float8_e4m3fn, 7), "e5m2": (ml_dtypes.float8_e5m2, 14)}[fmt]
    v = np.moveaxis(np.asarray(x, np.float32).astype(ml_dtypes.bfloat16).astype(np.float64), axis, -1)
    blocks = v.reshape(v.shape[:-1] + (-1, 32))
    amax = np.abs(blocks).max(-1, keepdims=True)
    byte = np.maximum(np.where(amax > 0, np.frexp(amax)[1] - 1 + 127, 0) - down, 1)
    scale = np.exp2(byte - 127.0)
    codes = (blocks / scale).astype(np.float32).astype(dtype).astype(np.float64)
    return np.moveaxis((codes * scale).reshape(v.shape), -1, axis)


WIDE = False


def mx_kscale(k):
    if not WIDE:
        return np.ones(k)
    levels = np.array([10, -10, 5, -5, 0])
    if k % 512:
        return np.exp2(np.random.permutation(np.resize(levels, k // 32))).repeat(32)
    a = np.empty((k // 512, 16))
    for p in range(k // 512):
        a[p, :8] = np.random.permutation(np.resize(levels, 8))
        for g in range(8):
            far = levels[np.abs(levels - a[p, g]) >= 10]
            a[p, g + 8] = far[np.random.randint(len(far))]
    return np.exp2(a.ravel()).repeat(32)


BF16 = ml_dtypes.bfloat16


def bf(x):
    return np.asarray(x, np.float32).astype(BF16)


def f64(x):
    return np.asarray(x).astype(np.float64)


B, N, L, H, S, R, C = 2, 512, 12, 64, 2, 2, 512
M = R * S * H
BN_EPS = 1e-5


def setup_inputs():
    s = mx_kscale(L * M).reshape(L, M)
    t = mx_kscale(C)
    return {"hops": bf((1.7 * np.random.standard_normal((B, N, L, M)) + 0.4 * np.random.standard_normal((L, M))) * s),
            "weight": bf(np.random.standard_normal((L, M, C)) * 0.6 / np.sqrt(L * M) / s[:, :, None]),
            "gamma": bf((1.0 + 0.1 * np.random.standard_normal(C)) * t),
            "beta": bf(0.2 * np.random.standard_normal(C) * t),
            "w2": bf(np.random.standard_normal((C, C)) / np.sqrt(C) / t[None, :]),
            "b2": bf(0.2 * np.random.standard_normal(C))}


def reference(hops, weight, gamma, beta, w2, b2):
    hf = f64(hops).reshape(B * N, L * M)
    wm = f64(weight).reshape(L * M, C)
    flat = mxq(hf, 1, "e4m3") @ mxq(wm, 0, "e4m3")
    mean = flat.mean(axis=0)
    var = flat.var(axis=0)
    normed = (flat - mean) * (1.0 / np.sqrt(var + BN_EPS)) * f64(gamma) + f64(beta)
    y = np.maximum(normed, 0.0)
    out = (mxq(y, 1, "e4m3") @ mxq(f64(w2), 1, "e4m3").T) + f64(b2)
    return out.reshape(B, N, C)

@@ -1,0 +1,332 @@
+from contextlib import ExitStack
+
+import concourse.mybir as mybir
+from concourse.masks import make_identity
+
+F32 = mybir.dt.float32
+BF16 = mybir.dt.bfloat16
+U32 = mybir.dt.uint32
+U8 = mybir.dt.uint8
+FP8X4 = mybir.dt.float8_e4m3fn_x4
+ACT = mybir.ActivationFunctionType
+ALU = mybir.AluOpType
+
+P = 128
+ROWS = 1024
+K1 = 3072
+C = 512
+PASSES = K1 // 512
+EPS = 1e-5
+EARLY_W = (4,)
+FLOPS = 2 * ROWS * K1 * C + 2 * ROWS * C * C
+
+
+def tile_ginconvfft_pb_kernel(tc, hops, weight, gamma, beta, w2, b2, out):
+    nc = tc.nc
+    hf = hops.rearrange("b n l m -> (b n) (l m)")
+    wm = weight.rearrange("l m c -> (l m) c")
+    of = out.rearrange("b n c -> (b n) c")
+
+    with ExitStack() as ctx:
+        keep = ctx.enter_context(tc.tile_pool(name="keep", bufs=1))
+        ring = ctx.enter_context(tc.tile_pool(name="ring", bufs=2))
+        psum = ctx.enter_context(tc.psum_pool(name="psum", bufs=1))
+        ctx.enter_context(tc.manual_schedule())
+
+        eps = keep.tile([P, 1], F32, name="eps")
+        warm = keep.tile([P, 1], F32, name="warm")
+        ident_f = keep.tile([P, P], F32, name="ident_f")
+        ident_b = keep.tile([P, P], BF16, name="ident_b")
+        ones = keep.tile([P, P], BF16, name="ones")
+        gam = keep.tile([P, 4], BF16, name="gam")
+        bet = keep.tile([P, 4], BF16, name="bet")
+        bz = keep.tile([P, C], BF16, name="bz")
+        hraw = [keep.tile([P, K1], BF16, name="hraw%d" % i) for i in range(8)]
+        w2raw = keep.tile([P, 4 * C], BF16, name="w2raw")
+        wraw = [keep.tile([P, 4 * C], BF16, name="wraw%d" % g) for g in range(PASSES)]
+        wg = [keep.tile([P, 4 * C], BF16, name="wg%d" % g, align_bytes=64) for g in range(PASSES)]
+        hc = keep.tile([P, PASSES * ROWS], U32, name="hc", align_bytes=64)
+        hs = keep.tile([P, PASSES * ROWS], U8, name="hs", align_bytes=64)
+        wc = keep.tile([P, PASSES * C], U32, name="wc", align_bytes=64)
+        ws = keep.tile([P, PASSES * C], U8, name="ws", align_bytes=64)
+        w2g = keep.tile([P, 4 * C], BF16, name="w2g", align_bytes=64)
+        w2c = keep.tile([P, C], U32, name="w2c", align_bytes=64)
+        w2s = keep.tile([P, C], U8, name="w2s", align_bytes=64)
+        yp = keep.tile([P, 4 * ROWS], BF16, name="yp")
+        yg = keep.tile([P, 4 * ROWS], BF16, name="yg", align_bytes=64)
+        yc = keep.tile([P, ROWS], U32, name="yc", align_bytes=64)
+        ys = keep.tile([P, ROWS], U8, name="ys", align_bytes=64)
+        b2bc = keep.tile([P, C], F32, name="b2bc")
+        gbf = keep.tile([P, 8], F32, name="gbf")
+
+        for a in range(4):
+            nc.sync.dma_start(out=w2raw[:, C * a : C * a + C], in_=w2[P * a : P * a + P, :])
+        def load_weights(g):
+            nc.sync.dma_start(
+                out=wraw[g][:], in_=wm[512 * g : 512 * g + 512, :].rearrange("(q e) c -> q (e c)", e=4)
+            )
+
+        for i in range(8):
+            if i in EARLY_W:
+                load_weights(EARLY_W.index(i))
+            pieces = 3 if i == 0 else 1
+            width = K1 // pieces
+            for s in range(pieces):
+                nc.sync.dma_start(
+                    out=hraw[i][:, width * s : width * s + width],
+                    in_=hf[P * i : P * i + P, width * s : width * s + width],
+                )
+        for g in range(len(EARLY_W), PASSES):
+            load_weights(g)
+        make_identity(nc, ident_b[:])
+        make_identity(nc, ident_f[:])
+        nc.vector.memset(bz[:], 0.0)
+        nc.vector.memset(eps[:], EPS)
+        nc.vector.memset(ones[:], 1.0)
+        nc.scalar.dma_start(out=gam[:], in_=gamma.rearrange("(p t) -> p t", t=4))
+        nc.scalar.dma_start(out=bet[:], in_=beta.rearrange("(p t) -> p t", t=4))
+        nc.scalar.dma_start(out=bz[0:1, :], in_=b2.rearrange("(o c) -> o c", o=1))
+        nc.scalar.activation(out=warm[:], in_=eps[:], func=ACT.Sqrt)
+
+        ring_count = [0]
+
+        def ring_bank():
+            n = ring_count[0]
+            ring_count[0] = n + 1
+            return "bank%d" % (4 + n % 4)
+
+        def w2_prepare():
+            for ap in range(2):
+                xw = psum.tile([P, 1024], BF16, name="xw", tag=ring_bank())
+                for a2 in range(2):
+                    for t in range(4):
+                        a = 2 * ap + a2
+                        k = 4 * a2 + t
+                        nc.tensor.transpose(
+                            xw[:, P * k : P * k + P],
+                            w2raw[:, C * a + t : C * a + C : 4],
+                            ident_b[:],
+                        )
+                nc.vector.tensor_copy(
+                    out=w2g[:, 1024 * ap : 1024 * ap + 1024].rearrange("p (a o t) -> p a o t", a=2, t=4),
+                    in_=xw[:].rearrange("p (a t o) -> p a o t", a=2, t=4),
+                )
+
+        G = {}
+
+        def transpose_tile(i, vector_banks):
+            j, ii = divmod(i, 2)
+            words = hraw[i][:].bitcast(F32)
+            for gp in range(3):
+                if ii == 0:
+                    G[(j, gp)] = ring.tile([P, 2048], BF16, name="G%d" % gp, align_bytes=64)
+                xt = psum.tile([P, 512], F32, name="xt", tag=ring_bank())
+                for k in range(4):
+                    w0 = 512 * gp + 256 * (k // 2)
+                    nc.tensor.transpose(xt[:, P * k : P * k + P], words[:, w0 + k % 2 : w0 + 256 : 2], ident_f[:])
+                dst = G[(j, gp)][:].bitcast(F32).rearrange("p (g r u) -> p g r u", g=2, u=2)
+                dst = dst[:, :, P * ii : P * ii + P, :]
+                src = xt[:].rearrange("p (g u r) -> p g r u", g=2, u=2)
+                if gp in vector_banks:
+                    nc.vector.tensor_copy(out=dst, in_=src)
+                else:
+                    nc.scalar.copy(out=dst, in_=src)
+
+        def q_hops(j, g):
+            gp, g2 = divmod(g, 2)
+            c0 = g * ROWS + 256 * j
+            nc.vector.quantize_mx(
+                out=hc[:, c0 : c0 + 256].bitcast(FP8X4),
+                scales=hs[:, c0 : c0 + 256],
+                in_=G[(j, gp)][:, 1024 * g2 : 1024 * g2 + 1024],
+            )
+
+        def regroup(eng_copy, dst_flat, src_planes):
+            eng_copy(
+                out=dst_flat.rearrange("p (c i t) -> p c t i", i=4, t=4),
+                in_=src_planes.rearrange("p t (c i) -> p c t i", i=4),
+            )
+
+        def r_w(eng_copy, g, a):
+            eng_copy(
+                out=wg[g][:, 1024 * a : 1024 * a + 1024].rearrange("p (t m j) -> p t m j", t=2, j=4),
+                in_=wraw[g][:].rearrange("p (j m t) -> p t m j", j=4, t=4)[:, 2 * a : 2 * a + 2, :, :],
+            )
+
+        def q_w(g):
+            nc.vector.quantize_mx(
+                out=wc[:, g * C : g * C + C].bitcast(FP8X4), scales=ws[:, g * C : g * C + C], in_=wg[g][:]
+            )
+
+        z = {}
+
+        def mx1(t, h, g):
+            if g == 0:
+                z[(t, h)] = psum.tile([P, 512], F32, name="z%d%d" % (t, h), tag="bank%d" % (4 * h + t))
+            nc.tensor.matmul_mx(
+                out=z[(t, h)][:],
+                lhsT=wc[:, g * C + P * t : g * C + P * t + P].bitcast(FP8X4),
+                lhsT_scale=ws[:, g * C + P * t : g * C + P * t + P],
+                rhs=hc[:, g * ROWS + 512 * h : g * ROWS + 512 * h + 512].bitcast(FP8X4),
+                rhs_scale=hs[:, g * ROWS + 512 * h : g * ROWS + 512 * h + 512],
+                start=(g == 0),
+                stop=(g == PASSES - 1),
+            )
+
+        stats = [keep.tile([P, 12], F32, name="stats%d" % t) for t in range(4)]
+        mv = [keep.tile([P, 2], F32, name="mv%d" % t) for t in range(4)]
+        std = [keep.tile([P, 1], F32, name="std%d" % t) for t in range(4)]
+        nmean = [keep.tile([P, 1], F32, name="nmean%d" % t) for t in range(4)]
+        rstd = [keep.tile([P, 1], F32, name="rstd%d" % t) for t in range(4)]
+        scl = [keep.tile([P, 1], F32, name="scl%d" % t) for t in range(4)]
+        bia = [keep.tile([P, 1], F32, name="bia%d" % t) for t in range(4)]
+
+        def bn_stat(t, h):
+            nc.vector.bn_stats(out=stats[t][:, 6 * h : 6 * h + 6], in_=z[(t, h)][:])
+
+        def bn_head(t):
+            nc.vector.bn_aggr(out=mv[t][:], in_=stats[t][:])
+            nc.scalar.activation(out=std[t][:], in_=mv[t][:, 1:2], func=ACT.Sqrt, bias=eps[:], scale=1.0)
+            nc.vector.tensor_scalar(out=nmean[t][:], in0=mv[t][:, 0:1], scalar1=-1.0, scalar2=None, op0=ALU.mult)
+
+        def bn_tail(t):
+            nc.vector.reciprocal(out=rstd[t][:], in_=std[t][:])
+            nc.vector.tensor_scalar(
+                out=scl[t][:], in0=rstd[t][:], scalar1=gbf[:, t : t + 1], scalar2=None, op0=ALU.mult
+            )
+            nc.vector.tensor_scalar(
+                out=bia[t][:],
+                in0=nmean[t][:],
+                scalar1=scl[t][:],
+                scalar2=gbf[:, 4 + t : 5 + t],
+                op0=ALU.mult,
+                op1=ALU.add,
+            )
+
+        def norm(t, r0, n):
+            h, c0 = divmod(r0, 512)
+            nc.scalar.activation(
+                out=yp[:, ROWS * t + r0 : ROWS * t + r0 + n],
+                in_=z[(t, h)][:, c0 : c0 + n],
+                func=ACT.Relu,
+                bias=bia[t][:],
+                scale=scl[t][:],
+            )
+
+        def affine_on_vector(t, r0, n):
+            h, c0 = divmod(r0, 512)
+            nc.vector.tensor_scalar(
+                out=yp[:, ROWS * t + r0 : ROWS * t + r0 + n],
+                in0=z[(t, h)][:, c0 : c0 + n],
+                scalar1=scl[t][:],
+                scalar2=bia[t][:],
+                op0=ALU.mult,
+                op1=ALU.add,
+            )
+
+        def relu_copy(out, in_):
+            nc.vector.tensor_scalar(out=out, in0=in_, scalar1=0.0, scalar2=None, op0=ALU.max)
+
+        def r_y(eng_copy, rc):
+            regroup(
+                eng_copy,
+                yg[:, 1024 * rc : 1024 * rc + 1024],
+                yp[:].rearrange("p (t x) -> p t x", t=4)[:, :, 256 * rc : 256 * rc + 256],
+            )
+
+        def q_y(rc):
+            nc.vector.quantize_mx(
+                out=yc[:, 256 * rc : 256 * rc + 256].bitcast(FP8X4),
+                scales=ys[:, 256 * rc : 256 * rc + 256],
+                in_=yg[:, 1024 * rc : 1024 * rc + 1024],
+            )
+
+        O_BANK = [0, 4, 1, 5, 2, 6, 3, 7]
+        ops = {}
+
+        def mx2(i):
+            ops[i] = psum.tile([P, C], F32, name="ops", tag="bank%d" % O_BANK[i])
+            nc.tensor.matmul_mx(
+                out=ops[i][:],
+                lhsT=yc[:, P * i : P * i + P].bitcast(FP8X4),
+                lhsT_scale=ys[:, P * i : P * i + P],
+                rhs=w2c[:].bitcast(FP8X4),
+                rhs_scale=w2s[:],
+                start=True,
+                stop=True,
+            )
+
+        ob = [keep.tile([P, C], F32, name="ob%d" % i) for i in range(8)]
+
+        def finish(i):
+            nc.vector.tensor_tensor(out=ob[i][:], in0=ops[i][:], in1=b2bc[:], op=ALU.add)
+            nc.sync.dma_start(out=of[P * i : P * i + P, :], in_=ob[i][:])
+
+        vcopy = nc.vector.tensor_copy
+        scopy = nc.scalar.copy
+
+        w2_prepare()
+        nc.vector.quantize_mx(out=w2c[:].bitcast(FP8X4), scales=w2s[:], in_=w2g[:])
+        for i in range(8):
+            transpose_tile(i, ())
+            if i == 2:
+                nc.vector.tensor_copy(out=gbf[:, 0:4], in_=gam[:])
+                nc.vector.tensor_copy(out=gbf[:, 4:8], in_=bet[:])
+                bps = psum.tile([P, C], F32, name="bps", tag=ring_bank())
+                nc.tensor.matmul(bps[:], lhsT=ones[:], rhs=bz[:], start=True, stop=True)
+                nc.vector.tensor_copy(out=b2bc[:], in_=bps[:])
+            if i in (1, 3, 5):
+                for g in range(PASSES):
+                    q_hops(i // 2, g)
+            if i in (3, 5):
+                g = (i - 3) // 2
+                r_w(vcopy, g, 0)
+                r_w(vcopy, g, 1)
+                q_w(g)
+
+        for g in range(2, PASSES):
+            r_w(scopy, g, 1)
+        r_w(vcopy, 2, 0)
+        for g in range(2, PASSES):
+            if g + 1 < PASSES:
+                r_w(vcopy, g + 1, 0)
+            q_w(g)
+        for g in range(PASSES):
+            q_hops(3, g)
+
+        for g in range(PASSES):
+            for t in range(4):
+                mx1(t, 0, g)
+        for t in range(4):
+            bn_stat(t, 0)
+
+        for t in range(4):
+            for g in range(PASSES):
+                mx1(t, 1, g)
+            bn_stat(t, 1)
+            bn_head(t)
+            if t > 0:
+                bn_tail(t - 1)
+                norm(t - 1, 0, 512)
+                norm(t - 1, 512, 512)
+        bn_tail(3)
+
+        affine_on_vector(3, 0, 256)
+        r_y(relu_copy, 0)
+        q_y(0)
+        for rc in range(1, 4):
+            norm(3, 256 * rc, 256)
+        r_y(vcopy, 1)
+        q_y(1)
+        r_y(scopy, 2)
+        r_y(scopy, 3)
+        for rc in range(4):
+            if rc > 1:
+                q_y(rc)
+            for i in (2 * rc, 2 * rc + 1):
+                mx2(i)
+            if rc > 0:
+                finish(2 * rc - 2)
+                finish(2 * rc - 1)
+        finish(6)
+        finish(7)

@@ -17,7 +17,6 @@ K1 = 3072
 C = 512
 PASSES = K1 // 512
 EPS = 1e-5
-EARLY_W = (4,)
 FLOPS = 2 * ROWS * K1 * C + 2 * ROWS * C * C
 
 
@@ -36,10 +35,12 @@ def tile_ginconvfft_pb_kernel(tc, hops, weight, gamma, beta, w2, b2, out):
         eps = keep.tile([P, 1], F32, name="eps")
         warm = keep.tile([P, 1], F32, name="warm")
         ident_f = keep.tile([P, P], F32, name="ident_f")
-        ident_b = keep.tile([P, P], BF16, name="ident_b")
         ones = keep.tile([P, P], BF16, name="ones")
         gam = keep.tile([P, 4], BF16, name="gam")
         bet = keep.tile([P, 4], BF16, name="bet")
+        gamf = keep.tile([P, 4], F32, name="gamf")
+        ngam = keep.tile([P, 4], F32, name="ngam")
+        betf = keep.tile([P, 4], F32, name="betf")
         bz = keep.tile([P, C], BF16, name="bz")
         hraw = [keep.tile([P, K1], BF16, name="hraw%d" % i) for i in range(8)]
         w2raw = keep.tile([P, 4 * C], BF16, name="w2raw")
@@ -57,36 +58,33 @@ def tile_ginconvfft_pb_kernel(tc, hops, weight, gamma, beta, w2, b2, out):
         yc = keep.tile([P, ROWS], U32, name="yc", align_bytes=64)
         ys = keep.tile([P, ROWS], U8, name="ys", align_bytes=64)
         b2bc = keep.tile([P, C], F32, name="b2bc")
-        gbf = keep.tile([P, 8], F32, name="gbf")
+        stats = [keep.tile([P, 12], F32, name="stats%d" % t) for t in range(4)]
+        mv = [keep.tile([P, 2], F32, name="mv%d" % t) for t in range(4)]
+        rstd = [keep.tile([P, 1], F32, name="rstd%d" % t) for t in range(4)]
+        mg = [keep.tile([P, 1], F32, name="mg%d" % t) for t in range(4)]
+        scl = [keep.tile([P, 1], F32, name="scl%d" % t) for t in range(4)]
+        bia = [keep.tile([P, 1], F32, name="bia%d" % t) for t in range(4)]
+        ob = [keep.tile([P, C], F32, name="ob%d" % i) for i in range(8)]
 
-        for a in range(4):
-            nc.sync.dma_start(out=w2raw[:, C * a : C * a + C], in_=w2[P * a : P * a + P, :])
+        vcopy = nc.vector.tensor_copy
+        scopy = nc.scalar.copy
+
+        def load_w2():
+            for a in range(4):
+                nc.sync.dma_start(out=w2raw[:, C * a : C * a + C], in_=w2[P * a : P * a + P, :])
+
         def load_weights(g):
             nc.sync.dma_start(
                 out=wraw[g][:], in_=wm[512 * g : 512 * g + 512, :].rearrange("(q e) c -> q (e c)", e=4)
             )
 
-        for i in range(8):
-            if i in EARLY_W:
-                load_weights(EARLY_W.index(i))
-            pieces = 3 if i == 0 else 1
+        def load_hops(i, pieces):
             width = K1 // pieces
             for s in range(pieces):
                 nc.sync.dma_start(
                     out=hraw[i][:, width * s : width * s + width],
                     in_=hf[P * i : P * i + P, width * s : width * s + width],
                 )
-        for g in range(len(EARLY_W), PASSES):
-            load_weights(g)
-        make_identity(nc, ident_b[:])
-        make_identity(nc, ident_f[:])
-        nc.vector.memset(bz[:], 0.0)
-        nc.vector.memset(eps[:], EPS)
-        nc.vector.memset(ones[:], 1.0)
-        nc.scalar.dma_start(out=gam[:], in_=gamma.rearrange("(p t) -> p t", t=4))
-        nc.scalar.dma_start(out=bet[:], in_=beta.rearrange("(p t) -> p t", t=4))
-        nc.scalar.dma_start(out=bz[0:1, :], in_=b2.rearrange("(o c) -> o c", o=1))
-        nc.scalar.activation(out=warm[:], in_=eps[:], func=ACT.Sqrt)
 
         ring_count = [0]
 
@@ -95,35 +93,59 @@ def tile_ginconvfft_pb_kernel(tc, hops, weight, gamma, beta, w2, b2, out):
             ring_count[0] = n + 1
             return "bank%d" % (4 + n % 4)
 
-        def w2_prepare():
-            for ap in range(2):
-                xw = psum.tile([P, 1024], BF16, name="xw", tag=ring_bank())
-                for a2 in range(2):
-                    for t in range(4):
-                        a = 2 * ap + a2
-                        k = 4 * a2 + t
-                        nc.tensor.transpose(
-                            xw[:, P * k : P * k + P],
-                            w2raw[:, C * a + t : C * a + C : 4],
-                            ident_b[:],
-                        )
-                nc.vector.tensor_copy(
-                    out=w2g[:, 1024 * ap : 1024 * ap + 1024].rearrange("p (a o t) -> p a o t", a=2, t=4),
-                    in_=xw[:].rearrange("p (a t o) -> p a o t", a=2, t=4),
-                )
+        def w2_transpose(ap, bank):
+            xw = psum.tile([P, 512], F32, name="xw", tag="bank%d" % bank)
+            words = w2raw[:].bitcast(F32)
+            for k in range(4):
+                w0 = 512 * ap + 256 * (k // 2)
+                nc.tensor.transpose(xw[:, P * k : P * k + P], words[:, w0 + k % 2 : w0 + 256 : 2], ident_f[:])
+            return xw
+
+        def w2_copy(eng_copy, ap, xw):
+            eng_copy(
+                out=w2g[:, 1024 * ap : 1024 * ap + 1024].bitcast(F32).rearrange("p (a o u) -> p a o u", a=2, u=2),
+                in_=xw[:].rearrange("p (a u o) -> p a o u", a=2, u=2),
+            )
+
+        def w2_quantize():
+            nc.vector.quantize_mx(out=w2c[:].bitcast(FP8X4), scales=w2s[:], in_=w2g[:])
+
+        def vectors_prepare():
+            nc.vector.tensor_copy(out=gamf[:], in_=gam[:])
+            nc.vector.tensor_copy(out=betf[:], in_=bet[:])
+            nc.vector.tensor_scalar(out=ngam[:], in0=gam[:], scalar1=-1.0, scalar2=None, op0=ALU.mult)
+
+        def b2_prepare(eng_copy):
+            bps = psum.tile([P, C], F32, name="bps", tag=ring_bank())
+            nc.tensor.matmul(bps[:], lhsT=ones[:], rhs=bz[:], start=True, stop=True)
+            eng_copy(out=b2bc[:], in_=bps[:])
 
         G = {}
+        hperm = {}
+
+        def permute_tile(i, pieces):
+            hperm[i] = ring.tile([P, K1], BF16, name="hperm")
+            width = K1 // 2 // pieces
+            for s in range(pieces):
+                nc.vector.tensor_copy(
+                    out=hperm[i][:].bitcast(F32)[:, width * s : width * s + width].rearrange("p (g u m) -> p g m u", u=2, m=P),
+                    in_=hraw[i][:].bitcast(F32)[:, width * s : width * s + width].rearrange("p (g m u) -> p g m u", u=2, m=P),
+                )
 
         def transpose_tile(i, vector_banks):
             j, ii = divmod(i, 2)
-            words = hraw[i][:].bitcast(F32)
+            words = (hperm[i] if i in hperm else hraw[i])[:].bitcast(F32)
             for gp in range(3):
                 if ii == 0:
                     G[(j, gp)] = ring.tile([P, 2048], BF16, name="G%d" % gp, align_bytes=64)
                 xt = psum.tile([P, 512], F32, name="xt", tag=ring_bank())
                 for k in range(4):
                     w0 = 512 * gp + 256 * (k // 2)
-                    nc.tensor.transpose(xt[:, P * k : P * k + P], words[:, w0 + k % 2 : w0 + 256 : 2], ident_f[:])
+                    if i in hperm:
+                        cols = words[:, 512 * gp + P * k : 512 * gp + P * k + P]
+                    else:
+                        cols = words[:, w0 + k % 2 : w0 + 256 : 2]
+                    nc.tensor.transpose(xt[:, P * k : P * k + P], cols, ident_f[:])
                 dst = G[(j, gp)][:].bitcast(F32).rearrange("p (g r u) -> p g r u", g=2, u=2)
                 dst = dst[:, :, P * ii : P * ii + P, :]
                 src = xt[:].rearrange("p (g u r) -> p g r u", g=2, u=2)
@@ -141,28 +163,30 @@ def tile_ginconvfft_pb_kernel(tc, hops, weight, gamma, beta, w2, b2, out):
                 in_=G[(j, gp)][:, 1024 * g2 : 1024 * g2 + 1024],
             )
 
-        def regroup(eng_copy, dst_flat, src_planes):
+        def warm_up(n):
+            for k in range(n):
+                d = psum.tile([P, C], F32, name="dummy", tag="bank3")
+                nc.tensor.matmul(d[:], lhsT=ones[:], rhs=bz[:], start=True, stop=True)
+
+        def r_w(eng_copy, g, t0, t1):
             eng_copy(
-                out=dst_flat.rearrange("p (c i t) -> p c t i", i=4, t=4),
-                in_=src_planes.rearrange("p t (c i) -> p c t i", i=4),
+                out=wg[g][:, 512 * t0 : 512 * t1].rearrange("p (t m j) -> p t m j", m=P, j=4),
+                in_=wraw[g][:].rearrange("p (j m t) -> p t m j", j=4, t=4)[:, t0:t1, :, :],
             )
 
-        def r_w(eng_copy, g, a):
-            eng_copy(
-                out=wg[g][:, 1024 * a : 1024 * a + 1024].rearrange("p (t m j) -> p t m j", t=2, j=4),
-                in_=wraw[g][:].rearrange("p (j m t) -> p t m j", j=4, t=4)[:, 2 * a : 2 * a + 2, :, :],
-            )
-
-        def q_w(g):
+        def q_w(g, a):
+            c0 = g * C + 256 * a
             nc.vector.quantize_mx(
-                out=wc[:, g * C : g * C + C].bitcast(FP8X4), scales=ws[:, g * C : g * C + C], in_=wg[g][:]
+                out=wc[:, c0 : c0 + 256].bitcast(FP8X4),
+                scales=ws[:, c0 : c0 + 256],
+                in_=wg[g][:, 1024 * a : 1024 * a + 1024],
             )
 
         z = {}
 
         def mx1(t, h, g):
             if g == 0:
-                z[(t, h)] = psum.tile([P, 512], F32, name="z%d%d" % (t, h), tag="bank%d" % (4 * h + t))
+                z[(t, h)] = psum.tile([P, 512], F32, name="z%d%d" % (t, h), tag="bank%d" % (2 * t + h))
             nc.tensor.matmul_mx(
                 out=z[(t, h)][:],
                 lhsT=wc[:, g * C + P * t : g * C + P * t + P].bitcast(FP8X4),
@@ -173,34 +197,24 @@ def tile_ginconvfft_pb_kernel(tc, hops, weight, gamma, beta, w2, b2, out):
                 stop=(g == PASSES - 1),
             )
 
-        stats = [keep.tile([P, 12], F32, name="stats%d" % t) for t in range(4)]
-        mv = [keep.tile([P, 2], F32, name="mv%d" % t) for t in range(4)]
-        std = [keep.tile([P, 1], F32, name="std%d" % t) for t in range(4)]
-        nmean = [keep.tile([P, 1], F32, name="nmean%d" % t) for t in range(4)]
-        rstd = [keep.tile([P, 1], F32, name="rstd%d" % t) for t in range(4)]
-        scl = [keep.tile([P, 1], F32, name="scl%d" % t) for t in range(4)]
-        bia = [keep.tile([P, 1], F32, name="bia%d" % t) for t in range(4)]
-
         def bn_stat(t, h):
             nc.vector.bn_stats(out=stats[t][:, 6 * h : 6 * h + 6], in_=z[(t, h)][:])
 
-        def bn_head(t):
+        def bn_mean(t):
             nc.vector.bn_aggr(out=mv[t][:], in_=stats[t][:])
-            nc.scalar.activation(out=std[t][:], in_=mv[t][:, 1:2], func=ACT.Sqrt, bias=eps[:], scale=1.0)
-            nc.vector.tensor_scalar(out=nmean[t][:], in0=mv[t][:, 0:1], scalar1=-1.0, scalar2=None, op0=ALU.mult)
-
-        def bn_tail(t):
-            nc.vector.reciprocal(out=rstd[t][:], in_=std[t][:])
-            nc.vector.tensor_scalar(
-                out=scl[t][:], in0=rstd[t][:], scalar1=gbf[:, t : t + 1], scalar2=None, op0=ALU.mult
+            nc.scalar.activation(
+                out=rstd[t][:], in_=mv[t][:, 1:2], func=ACT.Abs_reciprocal_sqrt, bias=eps[:], scale=1.0
             )
+
+        def bn_mg(t):
             nc.vector.tensor_scalar(
-                out=bia[t][:],
-                in0=nmean[t][:],
-                scalar1=scl[t][:],
-                scalar2=gbf[:, 4 + t : 5 + t],
-                op0=ALU.mult,
-                op1=ALU.add,
+                out=mg[t][:], in0=mv[t][:, 0:1], scalar1=ngam[:, t : t + 1], scalar2=None, op0=ALU.mult
+            )
+
+        def bn_scale(t):
+            nc.scalar.activation(out=scl[t][:], in_=rstd[t][:], func=ACT.Copy, scale=gamf[:, t : t + 1])
+            nc.scalar.activation(
+                out=bia[t][:], in_=rstd[t][:], func=ACT.Identity, scale=mg[t][:], bias=betf[:, t : t + 1]
             )
 
         def norm(t, r0, n):
@@ -213,25 +227,12 @@ def tile_ginconvfft_pb_kernel(tc, hops, weight, gamma, beta, w2, b2, out):
                 scale=scl[t][:],
             )
 
-        def affine_on_vector(t, r0, n):
-            h, c0 = divmod(r0, 512)
-            nc.vector.tensor_scalar(
-                out=yp[:, ROWS * t + r0 : ROWS * t + r0 + n],
-                in0=z[(t, h)][:, c0 : c0 + n],
-                scalar1=scl[t][:],
-                scalar2=bia[t][:],
-                op0=ALU.mult,
-                op1=ALU.add,
-            )
-
-        def relu_copy(out, in_):
-            nc.vector.tensor_scalar(out=out, in0=in_, scalar1=0.0, scalar2=None, op0=ALU.max)
-
         def r_y(eng_copy, rc):
-            regroup(
-                eng_copy,
-                yg[:, 1024 * rc : 1024 * rc + 1024],
-                yp[:].rearrange("p (t x) -> p t x", t=4)[:, :, 256 * rc : 256 * rc + 256],
+            eng_copy(
+                out=yg[:, 1024 * rc : 1024 * rc + 1024].rearrange("p (c i t) -> p c t i", i=4, t=4),
+                in_=yp[:]
+                .rearrange("p (t x) -> p t x", t=4)[:, :, 256 * rc : 256 * rc + 256]
+                .rearrange("p t (c i) -> p c t i", i=4),
             )
 
         def q_y(rc):
@@ -241,7 +242,7 @@ def tile_ginconvfft_pb_kernel(tc, hops, weight, gamma, beta, w2, b2, out):
                 in_=yg[:, 1024 * rc : 1024 * rc + 1024],
             )
 
-        O_BANK = [0, 4, 1, 5, 2, 6, 3, 7]
+        O_BANK = [2, 3, 4, 5, 0, 1, 6, 7]
         ops = {}
 
         def mx2(i):
@@ -256,66 +257,112 @@ def tile_ginconvfft_pb_kernel(tc, hops, weight, gamma, beta, w2, b2, out):
                 stop=True,
             )
 
-        ob = [keep.tile([P, C], F32, name="ob%d" % i) for i in range(8)]
-
         def finish(i):
             nc.vector.tensor_tensor(out=ob[i][:], in0=ops[i][:], in1=b2bc[:], op=ALU.add)
             nc.sync.dma_start(out=of[P * i : P * i + P, :], in_=ob[i][:])
 
-        vcopy = nc.vector.tensor_copy
-        scopy = nc.scalar.copy
+        load_hops(0, 3)
+        load_hops(1, 1)
+        load_hops(2, 1)
+        load_hops(3, 1)
+        load_hops(4, 1)
+        load_hops(5, 1)
+        load_hops(6, 1)
+        load_hops(7, 1)
+        load_weights(0)
+        load_weights(1)
+        load_weights(2)
+        load_weights(3)
+        load_weights(4)
+        load_weights(5)
+        load_w2()
 
-        w2_prepare()
-        nc.vector.quantize_mx(out=w2c[:].bitcast(FP8X4), scales=w2s[:], in_=w2g[:])
+        make_identity(nc, ident_f[:])
+        nc.vector.memset(bz[:], 0.0)
+        nc.vector.memset(eps[:], EPS)
+        nc.vector.memset(ones[:], 1.0)
+        nc.scalar.dma_start(out=bz[0:1, :], in_=b2.rearrange("(o c) -> o c", o=1))
+        nc.scalar.dma_start(out=gam[:], in_=gamma.rearrange("(p t) -> p t", t=4))
+        nc.scalar.dma_start(out=bet[:], in_=beta.rearrange("(p t) -> p t", t=4))
+        nc.scalar.activation(out=warm[:], in_=eps[:], func=ACT.Abs_reciprocal_sqrt)
+
+        PERM = []
+        if 0 in PERM:
+            permute_tile(0, 3)
+        b2_prepare(scopy)
+        vectors_prepare()
         for i in range(8):
             transpose_tile(i, ())
-            if i == 2:
-                nc.vector.tensor_copy(out=gbf[:, 0:4], in_=gam[:])
-                nc.vector.tensor_copy(out=gbf[:, 4:8], in_=bet[:])
-                bps = psum.tile([P, C], F32, name="bps", tag=ring_bank())
-                nc.tensor.matmul(bps[:], lhsT=ones[:], rhs=bz[:], start=True, stop=True)
-                nc.vector.tensor_copy(out=b2bc[:], in_=bps[:])
-            if i in (1, 3, 5):
-                for g in range(PASSES):
-                    q_hops(i // 2, g)
-            if i in (3, 5):
-                g = (i - 3) // 2
-                r_w(vcopy, g, 0)
-                r_w(vcopy, g, 1)
-                q_w(g)
+            if i < 7 and i + 1 in PERM:
+                permute_tile(i + 1, 1)
+            pass
+            if i > 0 and i < 7:
+                j, half = divmod(i - 1, 2)
+                for g in range(3 * half, 3 * half + 3):
+                    q_hops(j, g)
 
-        for g in range(2, PASSES):
-            r_w(scopy, g, 1)
-        r_w(vcopy, 2, 0)
-        for g in range(2, PASSES):
-            if g + 1 < PASSES:
-                r_w(vcopy, g + 1, 0)
-            q_w(g)
+        r_w(vcopy, 0, 0, 2)
+        r_w(vcopy, 1, 0, 2)
+        q_w(0, 0)
+        q_hops(3, 0)
+        q_w(1, 0)
+        q_hops(3, 1)
         for g in range(PASSES):
-            q_hops(3, g)
+            r_w(scopy, g, 2, 4)
+            if g > 1:
+                q_w(g, 0)
+            if g + 2 < PASSES:
+                r_w(vcopy, g + 2, 0, 2)
+                q_hops(3, g + 2)
+            for h in range(2):
+                for t in range(2):
+                    mx1(t, h, g)
+        for g in range(PASSES):
+            q_w(g, 1)
 
         for g in range(PASSES):
-            for t in range(4):
-                mx1(t, 0, g)
-        for t in range(4):
-            bn_stat(t, 0)
-
-        for t in range(4):
+            for h in range(2):
+                mx1(2, h, g)
+        for h in range(2):
             for g in range(PASSES):
-                mx1(t, 1, g)
-            bn_stat(t, 1)
-            bn_head(t)
-            if t > 0:
-                bn_tail(t - 1)
-                norm(t - 1, 0, 512)
-                norm(t - 1, 512, 512)
-        bn_tail(3)
+                mx1(3, h, g)
+        bn_stat(0, 0)
+        bn_stat(0, 1)
+        bn_stat(1, 0)
+        bn_mean(0)
+        bn_stat(1, 1)
+        bn_mg(0)
+        bn_scale(0)
+        norm(0, 0, 512)
+        bn_mean(1)
+        norm(0, 512, 512)
+        bn_stat(2, 0)
+        bn_mg(1)
+        bn_scale(1)
+        norm(1, 0, 512)
+        norm(1, 512, 512)
+        bn_stat(2, 1)
+        bn_stat(3, 0)
+        bn_mean(2)
+        bn_mg(2)
+        bn_scale(2)
+        norm(2, 0, 512)
+        xa = w2_transpose(0, 0)
+        xb = w2_transpose(1, 1)
+        norm(2, 512, 512)
+        w2_copy(scopy, 0, xa)
+        bn_stat(3, 1)
+        bn_mean(3)
+        bn_mg(3)
+        bn_scale(3)
+        w2_copy(vcopy, 1, xb)
 
-        affine_on_vector(3, 0, 256)
-        r_y(relu_copy, 0)
+        norm(3, 0, 256)
+        norm(3, 256, 256)
+        w2_quantize()
+        r_y(vcopy, 0)
+        norm(3, 512, 512)
         q_y(0)
-        for rc in range(1, 4):
-            norm(3, 256 * rc, 256)
         r_y(vcopy, 1)
         q_y(1)
         r_y(scopy, 2)

@@ -94,7 +94,7 @@ def tile_ginconvfft_pb_kernel(tc, hops, weight, gamma, beta, w2, b2, out):
             return "bank%d" % (4 + n % 4)
 
         def w2_transpose(ap, bank):
-            xw = psum.tile([P, 512], F32, name="xw", tag="bank%d" % bank)
+            xw = psum.tile([P, 512], F32, name="xw", tag=bank)
             words = w2raw[:].bitcast(F32)
             for k in range(4):
                 w0 = 512 * ap + 256 * (k // 2)
@@ -286,16 +286,11 @@ def tile_ginconvfft_pb_kernel(tc, hops, weight, gamma, beta, w2, b2, out):
         nc.scalar.dma_start(out=bet[:], in_=beta.rearrange("(p t) -> p t", t=4))
         nc.scalar.activation(out=warm[:], in_=eps[:], func=ACT.Abs_reciprocal_sqrt)
 
-        PERM = []
-        if 0 in PERM:
-            permute_tile(0, 3)
-        b2_prepare(scopy)
-        vectors_prepare()
         for i in range(8):
             transpose_tile(i, ())
-            if i < 7 and i + 1 in PERM:
-                permute_tile(i + 1, 1)
-            pass
+            if i == 2:
+                vectors_prepare()
+                b2_prepare(scopy)
             if i > 0 and i < 7:
                 j, half = divmod(i - 1, 2)
                 for g in range(3 * half, 3 * half + 3):
@@ -317,8 +312,18 @@ def tile_ginconvfft_pb_kernel(tc, hops, weight, gamma, beta, w2, b2, out):
             for h in range(2):
                 for t in range(2):
                     mx1(t, h, g)
-        for g in range(PASSES):
+        for g in range(4):
             q_w(g, 1)
+        bn_stat(0, 0)
+        bn_stat(0, 1)
+        q_w(4, 1)
+        bn_mean(0)
+        bn_stat(1, 0)
+        bn_mg(0)
+        bn_scale(0)
+        norm(0, 0, 512)
+        q_w(5, 1)
+        bn_stat(1, 1)
 
         for g in range(PASSES):
             for h in range(2):
@@ -326,31 +331,23 @@ def tile_ginconvfft_pb_kernel(tc, hops, weight, gamma, beta, w2, b2, out):
         for h in range(2):
             for g in range(PASSES):
                 mx1(3, h, g)
-        bn_stat(0, 0)
-        bn_stat(0, 1)
-        bn_stat(1, 0)
-        bn_mean(0)
-        bn_stat(1, 1)
-        bn_mg(0)
-        bn_scale(0)
-        norm(0, 0, 512)
-        bn_mean(1)
         norm(0, 512, 512)
-        bn_stat(2, 0)
+        bn_mean(1)
         bn_mg(1)
         bn_scale(1)
         norm(1, 0, 512)
         norm(1, 512, 512)
+        bn_stat(2, 0)
         bn_stat(2, 1)
-        bn_stat(3, 0)
         bn_mean(2)
         bn_mg(2)
         bn_scale(2)
         norm(2, 0, 512)
-        xa = w2_transpose(0, 0)
-        xb = w2_transpose(1, 1)
         norm(2, 512, 512)
+        bn_stat(3, 0)
+        xa = w2_transpose(0, "bank0")
         w2_copy(scopy, 0, xa)
+        xb = w2_transpose(1, "bank1")
         bn_stat(3, 1)
         bn_mean(3)
         bn_mg(3)

@@ -286,13 +286,18 @@ def tile_ginconvfft_pb_kernel(tc, hops, weight, gamma, beta, w2, b2, out):
         nc.scalar.dma_start(out=bet[:], in_=beta.rearrange("(p t) -> p t", t=4))
         nc.scalar.activation(out=warm[:], in_=eps[:], func=ACT.Abs_reciprocal_sqrt)
 
+        PERM = [0,1,2,3,4,5]
+        if 0 in PERM:
+            permute_tile(0, 3)
         for i in range(8):
             transpose_tile(i, ())
+            if i < 7 and i + 1 in PERM:
+                permute_tile(i + 1, 1)
             if i == 2:
                 vectors_prepare()
                 b2_prepare(scopy)
-            if i > 0 and i < 7:
-                j, half = divmod(i - 1, 2)
+            if i > 1 and i < 8:
+                j, half = divmod(i - 2, 2)
                 for g in range(3 * half, 3 * half + 3):
                     q_hops(j, g)
 

@@ -170,8 +170,8 @@ def tile_ginconvfft_pb_kernel(tc, hops, weight, gamma, beta, w2, b2, out):
 
         def r_w(eng_copy, g, t0, t1):
             eng_copy(
-                out=wg[g][:, 512 * t0 : 512 * t1].rearrange("p (t m j) -> p t m j", m=P, j=4),
-                in_=wraw[g][:].rearrange("p (j m t) -> p t m j", j=4, t=4)[:, t0:t1, :, :],
+                out=wg[g][:, 512 * t0 : 512 * t1].rearrange("p (t m j) -> p m j t", m=P, j=4),
+                in_=wraw[g][:].rearrange("p (j m t) -> p m j t", j=4, t=4)[:, :, :, t0:t1],
             )
 
         def q_w(g, a):

@@ -58,7 +58,7 @@ def tile_ginconvfft_pb_kernel(tc, hops, weight, gamma, beta, w2, b2, out):
         yc = keep.tile([P, ROWS], U32, name="yc", align_bytes=64)
         ys = keep.tile([P, ROWS], U8, name="ys", align_bytes=64)
         b2bc = keep.tile([P, C], F32, name="b2bc")
-        stats = [keep.tile([P, 12], F32, name="stats%d" % t) for t in range(4)]
+        stats = [keep.tile([P, 18 if t == 3 else 12], F32, name="stats%d" % t) for t in range(4)]
         mv = [keep.tile([P, 2], F32, name="mv%d" % t) for t in range(4)]
         rstd = [keep.tile([P, 1], F32, name="rstd%d" % t) for t in range(4)]
         mg = [keep.tile([P, 1], F32, name="mg%d" % t) for t in range(4)]
@@ -107,8 +107,12 @@ def tile_ginconvfft_pb_kernel(tc, hops, weight, gamma, beta, w2, b2, out):
                 in_=xw[:].rearrange("p (a u o) -> p a o u", a=2, u=2),
             )
 
-        def w2_quantize():
-            nc.vector.quantize_mx(out=w2c[:].bitcast(FP8X4), scales=w2s[:], in_=w2g[:])
+        def w2_quantize(ap):
+            nc.vector.quantize_mx(
+                out=w2c[:, 256 * ap : 256 * ap + 256].bitcast(FP8X4),
+                scales=w2s[:, 256 * ap : 256 * ap + 256],
+                in_=w2g[:, 1024 * ap : 1024 * ap + 1024],
+            )
 
         def vectors_prepare():
             nc.vector.tensor_copy(out=gamf[:], in_=gam[:])
@@ -184,21 +188,25 @@ def tile_ginconvfft_pb_kernel(tc, hops, weight, gamma, beta, w2, b2, out):
 
         z = {}
 
-        def mx1(t, h, g):
-            if g == 0:
+        def mx1(t, h, g, c0=0, n=512):
+            if g == 0 and c0 == 0:
                 z[(t, h)] = psum.tile([P, 512], F32, name="z%d%d" % (t, h), tag="bank%d" % (2 * t + h))
+            r0 = g * ROWS + 512 * h + c0
             nc.tensor.matmul_mx(
-                out=z[(t, h)][:],
+                out=z[(t, h)][:, c0 : c0 + n],
                 lhsT=wc[:, g * C + P * t : g * C + P * t + P].bitcast(FP8X4),
                 lhsT_scale=ws[:, g * C + P * t : g * C + P * t + P],
-                rhs=hc[:, g * ROWS + 512 * h : g * ROWS + 512 * h + 512].bitcast(FP8X4),
-                rhs_scale=hs[:, g * ROWS + 512 * h : g * ROWS + 512 * h + 512],
+                rhs=hc[:, r0 : r0 + n].bitcast(FP8X4),
+                rhs_scale=hs[:, r0 : r0 + n],
                 start=(g == 0),
                 stop=(g == PASSES - 1),
             )
 
         def bn_stat(t, h):
             nc.vector.bn_stats(out=stats[t][:, 6 * h : 6 * h + 6], in_=z[(t, h)][:])
+
+        def bn_stat_quarter(k):
+            nc.vector.bn_stats(out=stats[3][:, 6 + 6 * k : 12 + 6 * k], in_=z[(3, 1)][:, 256 * k : 256 * k + 256])
 
         def bn_mean(t):
             nc.vector.bn_aggr(out=mv[t][:], in_=stats[t][:])
@@ -227,19 +235,17 @@ def tile_ginconvfft_pb_kernel(tc, hops, weight, gamma, beta, w2, b2, out):
                 scale=scl[t][:],
             )
 
-        def r_y(eng_copy, rc):
+        def r_y(eng_copy, r0, n):
             eng_copy(
-                out=yg[:, 1024 * rc : 1024 * rc + 1024].rearrange("p (c i t) -> p c t i", i=4, t=4),
+                out=yg[:, 4 * r0 : 4 * (r0 + n)].rearrange("p (c i t) -> p c t i", i=4, t=4),
                 in_=yp[:]
-                .rearrange("p (t x) -> p t x", t=4)[:, :, 256 * rc : 256 * rc + 256]
+                .rearrange("p (t x) -> p t x", t=4)[:, :, r0 : r0 + n]
                 .rearrange("p t (c i) -> p c t i", i=4),
             )
 
-        def q_y(rc):
+        def q_y(r0, n):
             nc.vector.quantize_mx(
-                out=yc[:, 256 * rc : 256 * rc + 256].bitcast(FP8X4),
-                scales=ys[:, 256 * rc : 256 * rc + 256],
-                in_=yg[:, 1024 * rc : 1024 * rc + 1024],
+                out=yc[:, r0 : r0 + n].bitcast(FP8X4), scales=ys[:, r0 : r0 + n], in_=yg[:, 4 * r0 : 4 * (r0 + n)]
             )
 
         O_BANK = [2, 3, 4, 5, 0, 1, 6, 7]
@@ -256,6 +262,15 @@ def tile_ginconvfft_pb_kernel(tc, hops, weight, gamma, beta, w2, b2, out):
                 start=True,
                 stop=True,
             )
+
+        ot = [keep.tile([P, C], F32, name="ot%d" % i) for i in range(2)]
+
+        def empty_by_scalar(i):
+            nc.scalar.copy(out=ot[i % 2][:], in_=ops[i][:])
+
+        def add_by_gpsimd(i):
+            nc.gpsimd.tensor_tensor(out=ob[i][:], in0=ot[i % 2][:], in1=b2bc[:], op=ALU.add)
+            nc.scalar.dma_start(out=of[P * i : P * i + P, :], in_=ob[i][:])
 
         def finish(i):
             nc.vector.tensor_tensor(out=ob[i][:], in0=ops[i][:], in1=b2bc[:], op=ALU.add)
@@ -301,8 +316,11 @@ def tile_ginconvfft_pb_kernel(tc, hops, weight, gamma, beta, w2, b2, out):
                 for g in range(3 * half, 3 * half + 3):
                     q_hops(j, g)
 
+        S_EARLY = (2,)
         r_w(vcopy, 0, 0, 2)
         r_w(vcopy, 1, 0, 2)
+        for g in S_EARLY:
+            r_w(scopy, g, 0, 2)
         q_w(0, 0)
         q_hops(3, 0)
         q_w(1, 0)
@@ -312,7 +330,8 @@ def tile_ginconvfft_pb_kernel(tc, hops, weight, gamma, beta, w2, b2, out):
             if g > 1:
                 q_w(g, 0)
             if g + 2 < PASSES:
-                r_w(vcopy, g + 2, 0, 2)
+                if g + 2 not in S_EARLY:
+                    r_w(vcopy, g + 2, 0, 2)
                 q_hops(3, g + 2)
             for h in range(2):
                 for t in range(2):
@@ -333,9 +352,11 @@ def tile_ginconvfft_pb_kernel(tc, hops, weight, gamma, beta, w2, b2, out):
         for g in range(PASSES):
             for h in range(2):
                 mx1(2, h, g)
-        for h in range(2):
+        for g in range(PASSES):
+            mx1(3, 0, g)
+        for k in range(2):
             for g in range(PASSES):
-                mx1(3, h, g)
+                mx1(3, 1, g, 256 * k, 256)
         norm(0, 512, 512)
         bn_mean(1)
         bn_mg(1)
@@ -350,32 +371,42 @@ def tile_ginconvfft_pb_kernel(tc, hops, weight, gamma, beta, w2, b2, out):
         norm(2, 0, 512)
         norm(2, 512, 512)
         bn_stat(3, 0)
+        bn_stat_quarter(0)
         xa = w2_transpose(0, "bank0")
         w2_copy(scopy, 0, xa)
         xb = w2_transpose(1, "bank1")
-        bn_stat(3, 1)
+        bn_stat_quarter(1)
         bn_mean(3)
         bn_mg(3)
         bn_scale(3)
         w2_copy(vcopy, 1, xb)
 
-        norm(3, 0, 256)
-        norm(3, 256, 256)
-        w2_quantize()
-        r_y(vcopy, 0)
+        w2_quantize(0)
+        norm(3, 0, 128)
+        r_y(vcopy, 0, 128)
+        norm(3, 128, 384)
+        w2_quantize(1)
+        q_y(0, 128)
+        r_y(vcopy, 128, 128)
         norm(3, 512, 512)
-        q_y(0)
-        r_y(vcopy, 1)
-        q_y(1)
-        r_y(scopy, 2)
-        r_y(scopy, 3)
-        for rc in range(4):
-            if rc > 1:
-                q_y(rc)
-            for i in (2 * rc, 2 * rc + 1):
-                mx2(i)
-            if rc > 0:
-                finish(2 * rc - 2)
-                finish(2 * rc - 1)
-        finish(6)
-        finish(7)
+        r_y(vcopy, 256, 256)
+        q_y(128, 128)
+        mx2(0)
+        mx2(1)
+        r_y(scopy, 512, 256)
+        r_y(scopy, 768, 256)
+        finish(0)
+        q_y(256, 256)
+        mx2(2)
+        mx2(3)
+        finish(1)
+        q_y(512, 256)
+        mx2(4)
+        mx2(5)
+        finish(2)
+        finish(3)
+        q_y(768, 256)
+        mx2(6)
+        mx2(7)
+        for i in range(4, 8):
+            finish(i)

@@ -119,10 +119,10 @@ def tile_ginconvfft_pb_kernel(tc, hops, weight, gamma, beta, w2, b2, out):
             nc.vector.tensor_copy(out=betf[:], in_=bet[:])
             nc.vector.tensor_scalar(out=ngam[:], in0=gam[:], scalar1=-1.0, scalar2=None, op0=ALU.mult)
 
-        def b2_prepare(eng_copy):
-            bps = psum.tile([P, C], F32, name="bps", tag=ring_bank())
+        def b2_spread():
+            bps = psum.tile([P, C], F32, name="bps", tag="bank4")
             nc.tensor.matmul(bps[:], lhsT=ones[:], rhs=bz[:], start=True, stop=True)
-            eng_copy(out=b2bc[:], in_=bps[:])
+            return bps
 
         G = {}
         hperm = {}
@@ -174,8 +174,8 @@ def tile_ginconvfft_pb_kernel(tc, hops, weight, gamma, beta, w2, b2, out):
 
         def r_w(eng_copy, g, t0, t1):
             eng_copy(
-                out=wg[g][:, 512 * t0 : 512 * t1].rearrange("p (t m j) -> p m j t", m=P, j=4),
-                in_=wraw[g][:].rearrange("p (j m t) -> p m j t", j=4, t=4)[:, :, :, t0:t1],
+                out=wg[g][:, 512 * t0 : 512 * t1].rearrange("p (t m i j) -> p m j t i", i=2, j=4, t=t1 - t0),
+                in_=wraw[g][:].rearrange("p (j m i t) -> p m j t i", j=4, i=2, t=4)[:, :, :, t0:t1, :],
             )
 
         def q_w(g, a):
@@ -308,9 +308,8 @@ def tile_ginconvfft_pb_kernel(tc, hops, weight, gamma, beta, w2, b2, out):
             transpose_tile(i, ())
             if i < 7 and i + 1 in PERM:
                 permute_tile(i + 1, 1)
-            if i == 2:
+            if i == 0:
                 vectors_prepare()
-                b2_prepare(scopy)
             if i > 1 and i < 8:
                 j, half = divmod(i - 2, 2)
                 for g in range(3 * half, 3 * half + 3):
@@ -326,7 +325,7 @@ def tile_ginconvfft_pb_kernel(tc, hops, weight, gamma, beta, w2, b2, out):
         q_w(1, 0)
         q_hops(3, 1)
         for g in range(PASSES):
-            r_w(scopy, g, 2, 4)
+            r_w(vcopy if g == 5 else scopy, g, 2, 4)
             if g > 1:
                 q_w(g, 0)
             if g + 2 < PASSES:
@@ -380,6 +379,7 @@ def tile_ginconvfft_pb_kernel(tc, hops, weight, gamma, beta, w2, b2, out):
         bn_mg(3)
         bn_scale(3)
         w2_copy(vcopy, 1, xb)
+        bps = b2_spread()
 
         w2_quantize(0)
         norm(3, 0, 128)
@@ -389,6 +389,7 @@ def tile_ginconvfft_pb_kernel(tc, hops, weight, gamma, beta, w2, b2, out):
         q_y(0, 128)
         r_y(vcopy, 128, 128)
         norm(3, 512, 512)
+        nc.scalar.copy(out=b2bc[:], in_=bps[:])
         r_y(vcopy, 256, 256)
         q_y(128, 128)
         mx2(0)

@@ -115,9 +115,9 @@ def tile_ginconvfft_pb_kernel(tc, hops, weight, gamma, beta, w2, b2, out):
             )
 
         def vectors_prepare():
-            nc.vector.tensor_copy(out=gamf[:], in_=gam[:])
-            nc.vector.tensor_copy(out=betf[:], in_=bet[:])
-            nc.vector.tensor_scalar(out=ngam[:], in0=gam[:], scalar1=-1.0, scalar2=None, op0=ALU.mult)
+            nc.gpsimd.tensor_copy(out=gamf[:], in_=gam[:])
+            nc.gpsimd.tensor_copy(out=betf[:], in_=bet[:])
+            nc.gpsimd.tensor_scalar(out=ngam[:], in0=gam[:], scalar1=-1.0, scalar2=None, op0=ALU.mult)
 
         def b2_spread():
             bps = psum.tile([P, C], F32, name="bps", tag="bank4")
@@ -290,15 +290,16 @@ def tile_ginconvfft_pb_kernel(tc, hops, weight, gamma, beta, w2, b2, out):
         load_weights(3)
         load_weights(4)
         load_weights(5)
+        nc.sync.dma_start(out=gam[:], in_=gamma.rearrange("(p t) -> p t", t=4))
+        nc.sync.dma_start(out=bet[:], in_=beta.rearrange("(p t) -> p t", t=4))
         load_w2()
+        nc.vector.memset(bz[:], 0.0)
+        nc.sync.dma_start(out=bz[0:1, :], in_=b2.rearrange("(o c) -> o c", o=1))
 
         make_identity(nc, ident_f[:])
-        nc.vector.memset(bz[:], 0.0)
+        vectors_prepare()
         nc.vector.memset(eps[:], EPS)
         nc.vector.memset(ones[:], 1.0)
-        nc.scalar.dma_start(out=bz[0:1, :], in_=b2.rearrange("(o c) -> o c", o=1))
-        nc.scalar.dma_start(out=gam[:], in_=gamma.rearrange("(p t) -> p t", t=4))
-        nc.scalar.dma_start(out=bet[:], in_=beta.rearrange("(p t) -> p t", t=4))
         nc.scalar.activation(out=warm[:], in_=eps[:], func=ACT.Abs_reciprocal_sqrt)
 
         PERM = [0,1,2,3,4,5]
@@ -308,8 +309,6 @@ def tile_ginconvfft_pb_kernel(tc, hops, weight, gamma, beta, w2, b2, out):
             transpose_tile(i, ())
             if i < 7 and i + 1 in PERM:
                 permute_tile(i + 1, 1)
-            if i == 0:
-                vectors_prepare()
             if i > 1 and i < 8:
                 j, half = divmod(i - 2, 2)
                 for g in range(3 * half, 3 * half + 3):

from contextlib import ExitStack

import concourse.mybir as mybir
from concourse.masks import make_identity

F32 = mybir.dt.float32
BF16 = mybir.dt.bfloat16
U32 = mybir.dt.uint32
U8 = mybir.dt.uint8
FP8X4 = mybir.dt.float8_e4m3fn_x4
ACT = mybir.ActivationFunctionType
ALU = mybir.AluOpType

P = 128
ROWS = 1024
K1 = 3072
C = 512
PASSES = K1 // 512
EPS = 1e-5
FLOPS = 2 * ROWS * K1 * C + 2 * ROWS * C * C


def tile_ginconvfft_pb_kernel(tc, hops, weight, gamma, beta, w2, b2, out):
    nc = tc.nc
    hf = hops.rearrange("b n l m -> (b n) (l m)")
    wm = weight.rearrange("l m c -> (l m) c")
    of = out.rearrange("b n c -> (b n) c")

    with ExitStack() as ctx:
        keep = ctx.enter_context(tc.tile_pool(name="keep", bufs=1))
        ring = ctx.enter_context(tc.tile_pool(name="ring", bufs=2))
        psum = ctx.enter_context(tc.psum_pool(name="psum", bufs=1))
        ctx.enter_context(tc.manual_schedule())

        eps = keep.tile([P, 1], F32, name="eps")
        warm = keep.tile([P, 1], F32, name="warm")
        ident_f = keep.tile([P, P], F32, name="ident_f")
        ones = keep.tile([P, P], BF16, name="ones")
        gam = keep.tile([P, 4], BF16, name="gam")
        bet = keep.tile([P, 4], BF16, name="bet")
        gamf = keep.tile([P, 4], F32, name="gamf")
        ngam = keep.tile([P, 4], F32, name="ngam")
        betf = keep.tile([P, 4], F32, name="betf")
        bz = keep.tile([P, C], BF16, name="bz")
        hraw = [keep.tile([P, K1], BF16, name="hraw%d" % i) for i in range(8)]
        w2raw = keep.tile([P, 4 * C], BF16, name="w2raw")
        wraw = [keep.tile([P, 4 * C], BF16, name="wraw%d" % g) for g in range(PASSES)]
        wg = [keep.tile([P, 4 * C], BF16, name="wg%d" % g, align_bytes=64) for g in range(PASSES)]
        hc = keep.tile([P, PASSES * ROWS], U32, name="hc", align_bytes=64)
        hs = keep.tile([P, PASSES * ROWS], U8, name="hs", align_bytes=64)
        wc = keep.tile([P, PASSES * C], U32, name="wc", align_bytes=64)
        ws = keep.tile([P, PASSES * C], U8, name="ws", align_bytes=64)
        w2g = keep.tile([P, 4 * C], BF16, name="w2g", align_bytes=64)
        w2c = keep.tile([P, C], U32, name="w2c", align_bytes=64)
        w2s = keep.tile([P, C], U8, name="w2s", align_bytes=64)
        yp = keep.tile([P, 4 * ROWS], BF16, name="yp")
        yg = keep.tile([P, 4 * ROWS], BF16, name="yg", align_bytes=64)
        yc = keep.tile([P, ROWS], U32, name="yc", align_bytes=64)
        ys = keep.tile([P, ROWS], U8, name="ys", align_bytes=64)
        b2bc = keep.tile([P, C], F32, name="b2bc")
        stats = [keep.tile([P, 18 if t == 3 else 12], F32, name="stats%d" % t) for t in range(4)]
        mv = [keep.tile([P, 2], F32, name="mv%d" % t) for t in range(4)]
        rstd = [keep.tile([P, 1], F32, name="rstd%d" % t) for t in range(4)]
        mg = [keep.tile([P, 1], F32, name="mg%d" % t) for t in range(4)]
        scl = [keep.tile([P, 1], F32, name="scl%d" % t) for t in range(4)]
        bia = [keep.tile([P, 1], F32, name="bia%d" % t) for t in range(4)]
        ob = [keep.tile([P, C], F32, name="ob%d" % i) for i in range(8)]

        vcopy = nc.vector.tensor_copy
        scopy = nc.scalar.copy

        def load_w2():
            for a in range(4):
                nc.sync.dma_start(out=w2raw[:, C * a : C * a + C], in_=w2[P * a : P * a + P, :])

        def load_weights(g):
            nc.sync.dma_start(
                out=wraw[g][:], in_=wm[512 * g : 512 * g + 512, :].rearrange("(q e) c -> q (e c)", e=4)
            )

        def load_hops(i, pieces):
            width = K1 // pieces
            for s in range(pieces):
                nc.sync.dma_start(
                    out=hraw[i][:, width * s : width * s + width],
                    in_=hf[P * i : P * i + P, width * s : width * s + width],
                )

        ring_count = [0]

        def ring_bank():
            n = ring_count[0]
            ring_count[0] = n + 1
            return "bank%d" % (4 + n % 4)

        def w2_transpose(ap, bank):
            xw = psum.tile([P, 512], F32, name="xw", tag=bank)
            words = w2raw[:].bitcast(F32)
            for k in range(4):
                w0 = 512 * ap + 256 * (k // 2)
                nc.tensor.transpose(xw[:, P * k : P * k + P], words[:, w0 + k % 2 : w0 + 256 : 2], ident_f[:])
            return xw

        def w2_copy(eng_copy, ap, xw):
            eng_copy(
                out=w2g[:, 1024 * ap : 1024 * ap + 1024].bitcast(F32).rearrange("p (a o u) -> p a o u", a=2, u=2),
                in_=xw[:].rearrange("p (a u o) -> p a o u", a=2, u=2),
            )

        def w2_quantize(ap):
            nc.vector.quantize_mx(
                out=w2c[:, 256 * ap : 256 * ap + 256].bitcast(FP8X4),
                scales=w2s[:, 256 * ap : 256 * ap + 256],
                in_=w2g[:, 1024 * ap : 1024 * ap + 1024],
            )

        def vectors_prepare():
            nc.gpsimd.tensor_copy(out=gamf[:], in_=gam[:])
            nc.gpsimd.tensor_copy(out=betf[:], in_=bet[:])
            nc.gpsimd.tensor_scalar(out=ngam[:], in0=gam[:], scalar1=-1.0, scalar2=None, op0=ALU.mult)

        def b2_spread():
            bps = psum.tile([P, C], F32, name="bps", tag="bank4")
            nc.tensor.matmul(bps[:], lhsT=ones[:], rhs=bz[:], start=True, stop=True)
            return bps

        G = {}
        hperm = {}

        def permute_tile(i, pieces):
            hperm[i] = ring.tile([P, K1], BF16, name="hperm")
            width = K1 // 2 // pieces
            for s in range(pieces):
                nc.vector.tensor_copy(
                    out=hperm[i][:].bitcast(F32)[:, width * s : width * s + width].rearrange("p (g u m) -> p g m u", u=2, m=P),
                    in_=hraw[i][:].bitcast(F32)[:, width * s : width * s + width].rearrange("p (g m u) -> p g m u", u=2, m=P),
                )

        def transpose_tile(i, vector_banks):
            j, ii = divmod(i, 2)
            words = (hperm[i] if i in hperm else hraw[i])[:].bitcast(F32)
            for gp in range(3):
                if ii == 0:
                    G[(j, gp)] = ring.tile([P, 2048], BF16, name="G%d" % gp, align_bytes=64)
                xt = psum.tile([P, 512], F32, name="xt", tag=ring_bank())
                for k in range(4):
                    w0 = 512 * gp + 256 * (k // 2)
                    if i in hperm:
                        cols = words[:, 512 * gp + P * k : 512 * gp + P * k + P]
                    else:
                        cols = words[:, w0 + k % 2 : w0 + 256 : 2]
                    nc.tensor.transpose(xt[:, P * k : P * k + P], cols, ident_f[:])
                dst = G[(j, gp)][:].bitcast(F32).rearrange("p (g r u) -> p g r u", g=2, u=2)
                dst = dst[:, :, P * ii : P * ii + P, :]
                src = xt[:].rearrange("p (g u r) -> p g r u", g=2, u=2)
                if gp in vector_banks:
                    nc.vector.tensor_copy(out=dst, in_=src)
                else:
                    nc.scalar.copy(out=dst, in_=src)

        def q_hops(j, g):
            gp, g2 = divmod(g, 2)
            c0 = g * ROWS + 256 * j
            nc.vector.quantize_mx(
                out=hc[:, c0 : c0 + 256].bitcast(FP8X4),
                scales=hs[:, c0 : c0 + 256],
                in_=G[(j, gp)][:, 1024 * g2 : 1024 * g2 + 1024],
            )

        def warm_up(n):
            for k in range(n):
                d = psum.tile([P, C], F32, name="dummy", tag="bank3")
                nc.tensor.matmul(d[:], lhsT=ones[:], rhs=bz[:], start=True, stop=True)

        def r_w(eng_copy, g, t0, t1):
            eng_copy(
                out=wg[g][:, 512 * t0 : 512 * t1].rearrange("p (t m i j) -> p m j t i", i=2, j=4, t=t1 - t0),
                in_=wraw[g][:].rearrange("p (j m i t) -> p m j t i", j=4, i=2, t=4)[:, :, :, t0:t1, :],
            )

        def q_w(g, a):
            c0 = g * C + 256 * a
            nc.vector.quantize_mx(
                out=wc[:, c0 : c0 + 256].bitcast(FP8X4),
                scales=ws[:, c0 : c0 + 256],
                in_=wg[g][:, 1024 * a : 1024 * a + 1024],
            )

        z = {}

        def mx1(t, h, g, c0=0, n=512):
            if g == 0 and c0 == 0:
                z[(t, h)] = psum.tile([P, 512], F32, name="z%d%d" % (t, h), tag="bank%d" % (2 * t + h))
            r0 = g * ROWS + 512 * h + c0
            nc.tensor.matmul_mx(
                out=z[(t, h)][:, c0 : c0 + n],
                lhsT=wc[:, g * C + P * t : g * C + P * t + P].bitcast(FP8X4),
                lhsT_scale=ws[:, g * C + P * t : g * C + P * t + P],
                rhs=hc[:, r0 : r0 + n].bitcast(FP8X4),
                rhs_scale=hs[:, r0 : r0 + n],
                start=(g == 0),
                stop=(g == PASSES - 1),
            )

        def bn_stat(t, h):
            nc.vector.bn_stats(out=stats[t][:, 6 * h : 6 * h + 6], in_=z[(t, h)][:])

        def bn_stat_quarter(k):
            nc.vector.bn_stats(out=stats[3][:, 6 + 6 * k : 12 + 6 * k], in_=z[(3, 1)][:, 256 * k : 256 * k + 256])

        def bn_mean(t):
            nc.vector.bn_aggr(out=mv[t][:], in_=stats[t][:])
            nc.scalar.activation(
                out=rstd[t][:], in_=mv[t][:, 1:2], func=ACT.Abs_reciprocal_sqrt, bias=eps[:], scale=1.0
            )

        def bn_mg(t):
            nc.vector.tensor_scalar(
                out=mg[t][:], in0=mv[t][:, 0:1], scalar1=ngam[:, t : t + 1], scalar2=None, op0=ALU.mult
            )

        def bn_scale(t):
            nc.scalar.activation(out=scl[t][:], in_=rstd[t][:], func=ACT.Copy, scale=gamf[:, t : t + 1])
            nc.scalar.activation(
                out=bia[t][:], in_=rstd[t][:], func=ACT.Identity, scale=mg[t][:], bias=betf[:, t : t + 1]
            )

        def norm(t, r0, n):
            h, c0 = divmod(r0, 512)
            nc.scalar.activation(
                out=yp[:, ROWS * t + r0 : ROWS * t + r0 + n],
                in_=z[(t, h)][:, c0 : c0 + n],
                func=ACT.Relu,
                bias=bia[t][:],
                scale=scl[t][:],
            )

        def r_y(eng_copy, r0, n):
            eng_copy(
                out=yg[:, 4 * r0 : 4 * (r0 + n)].rearrange("p (c i t) -> p c t i", i=4, t=4),
                in_=yp[:]
                .rearrange("p (t x) -> p t x", t=4)[:, :, r0 : r0 + n]
                .rearrange("p t (c i) -> p c t i", i=4),
            )

        def q_y(r0, n):
            nc.vector.quantize_mx(
                out=yc[:, r0 : r0 + n].bitcast(FP8X4), scales=ys[:, r0 : r0 + n], in_=yg[:, 4 * r0 : 4 * (r0 + n)]
            )

        O_BANK = [2, 3, 4, 5, 0, 1, 6, 7]
        ops = {}

        def mx2(i):
            ops[i] = psum.tile([P, C], F32, name="ops", tag="bank%d" % O_BANK[i])
            nc.tensor.matmul_mx(
                out=ops[i][:],
                lhsT=yc[:, P * i : P * i + P].bitcast(FP8X4),
                lhsT_scale=ys[:, P * i : P * i + P],
                rhs=w2c[:].bitcast(FP8X4),
                rhs_scale=w2s[:],
                start=True,
                stop=True,
            )

        ot = [keep.tile([P, C], F32, name="ot%d" % i) for i in range(2)]

        def empty_by_scalar(i):
            nc.scalar.copy(out=ot[i % 2][:], in_=ops[i][:])

        def add_by_gpsimd(i):
            nc.gpsimd.tensor_tensor(out=ob[i][:], in0=ot[i % 2][:], in1=b2bc[:], op=ALU.add)
            nc.scalar.dma_start(out=of[P * i : P * i + P, :], in_=ob[i][:])

        def finish(i):
            nc.vector.tensor_tensor(out=ob[i][:], in0=ops[i][:], in1=b2bc[:], op=ALU.add)
            nc.sync.dma_start(out=of[P * i : P * i + P, :], in_=ob[i][:])

        load_hops(0, 3)
        load_hops(1, 1)
        load_hops(2, 1)
        load_hops(3, 1)
        load_hops(4, 1)
        load_hops(5, 1)
        load_hops(6, 1)
        load_hops(7, 1)
        load_weights(0)
        load_weights(1)
        load_weights(2)
        load_weights(3)
        load_weights(4)
        load_weights(5)
        nc.sync.dma_start(out=gam[:], in_=gamma.rearrange("(p t) -> p t", t=4))
        nc.sync.dma_start(out=bet[:], in_=beta.rearrange("(p t) -> p t", t=4))
        load_w2()
        nc.vector.memset(bz[:], 0.0)
        nc.sync.dma_start(out=bz[0:1, :], in_=b2.rearrange("(o c) -> o c", o=1))

        make_identity(nc, ident_f[:])
        vectors_prepare()
        nc.vector.memset(eps[:], EPS)
        nc.vector.memset(ones[:], 1.0)
        nc.scalar.activation(out=warm[:], in_=eps[:], func=ACT.Abs_reciprocal_sqrt)

        PERM = [0,1,2,3,4,5]
        if 0 in PERM:
            permute_tile(0, 3)
        for i in range(8):
            transpose_tile(i, ())
            if i < 7 and i + 1 in PERM:
                permute_tile(i + 1, 1)
            if i > 1 and i < 8:
                j, half = divmod(i - 2, 2)
                for g in range(3 * half, 3 * half + 3):
                    q_hops(j, g)

        S_EARLY = (2,)
        r_w(vcopy, 0, 0, 2)
        r_w(vcopy, 1, 0, 2)
        for g in S_EARLY:
            r_w(scopy, g, 0, 2)
        q_w(0, 0)
        q_hops(3, 0)
        q_w(1, 0)
        q_hops(3, 1)
        for g in range(PASSES):
            r_w(vcopy if g == 5 else scopy, g, 2, 4)
            if g > 1:
                q_w(g, 0)
            if g + 2 < PASSES:
                if g + 2 not in S_EARLY:
                    r_w(vcopy, g + 2, 0, 2)
                q_hops(3, g + 2)
            for h in range(2):
                for t in range(2):
                    mx1(t, h, g)
        for g in range(4):
            q_w(g, 1)
        bn_stat(0, 0)
        bn_stat(0, 1)
        q_w(4, 1)
        bn_mean(0)
        bn_stat(1, 0)
        bn_mg(0)
        bn_scale(0)
        norm(0, 0, 512)
        q_w(5, 1)
        bn_stat(1, 1)

        for g in range(PASSES):
            for h in range(2):
                mx1(2, h, g)
        for g in range(PASSES):
            mx1(3, 0, g)
        for k in range(2):
            for g in range(PASSES):
                mx1(3, 1, g, 256 * k, 256)
        norm(0, 512, 512)
        bn_mean(1)
        bn_mg(1)
        bn_scale(1)
        norm(1, 0, 512)
        norm(1, 512, 512)
        bn_stat(2, 0)
        bn_stat(2, 1)
        bn_mean(2)
        bn_mg(2)
        bn_scale(2)
        norm(2, 0, 512)
        norm(2, 512, 512)
        bn_stat(3, 0)
        bn_stat_quarter(0)
        xa = w2_transpose(0, "bank0")
        w2_copy(scopy, 0, xa)
        xb = w2_transpose(1, "bank1")
        bn_stat_quarter(1)
        bn_mean(3)
        bn_mg(3)
        bn_scale(3)
        w2_copy(vcopy, 1, xb)
        bps = b2_spread()

        w2_quantize(0)
        norm(3, 0, 128)
        r_y(vcopy, 0, 128)
        norm(3, 128, 384)
        w2_quantize(1)
        q_y(0, 128)
        r_y(vcopy, 128, 128)
        norm(3, 512, 512)
        nc.scalar.copy(out=b2bc[:], in_=bps[:])
        r_y(vcopy, 256, 256)
        q_y(128, 128)
        mx2(0)
        mx2(1)
        r_y(scopy, 512, 256)
        r_y(scopy, 768, 256)
        finish(0)
        q_y(256, 256)
        mx2(2)
        mx2(3)
        finish(1)
        q_y(512, 256)
        mx2(4)
        mx2(5)
        finish(2)
        finish(3)
        q_y(768, 256)
        mx2(6)
        mx2(7)
        for i in range(4, 8):
            finish(i)
